import numpy as np
import ml_dtypes


def mxq(x, axis, fmt="e4m3"):
    dtype, down = {"e4m3": (ml_dtypes.float8_e4m3fn, 7), "e5m2": (ml_dtypes.float8_e5m2, 14)}[fmt]
    v = np.moveaxis(np.asarray(x, np.float32).astype(ml_dtypes.bfloat16).astype(np.float64), axis, -1)
    blocks = v.reshape(v.shape[:-1] + (-1, 32))
    amax = np.abs(blocks).max(-1, keepdims=True)
    byte = np.maximum(np.where(amax > 0, np.frexp(amax)[1] - 1 + 127, 0) - down, 1)
    scale = np.exp2(byte - 127.0)
    codes = (blocks / scale).astype(np.float32).astype(dtype).astype(np.float64)
    return np.moveaxis((codes * scale).reshape(v.shape), -1, axis)


WIDE = False


def mx_kscale(k):
    if not WIDE:
        return np.ones(k)
    levels = np.array([10, -10, 5, -5, 0])
    a = np.random.permutation(np.resize(levels, k // 512 * 4)).reshape(k // 512, 4)
    idx = np.arange(k)
    return np.exp2(a[idx // 512, idx % 128 // 32])


BF16 = ml_dtypes.bfloat16


def bf(x):
    return np.asarray(x, np.float32).astype(BF16)


def f64(x):
    return np.asarray(x).astype(np.float64)


E2M1 = np.array([0.0, 0.5, 1.0, 1.5, 2.0, 3.0, 4.0, 6.0, -0.0, -0.5, -1.0, -1.5, -2.0, -3.0, -4.0, -6.0])


def pack_weight(w, fmt):
    k, n = w.shape
    w = f64(bf(w)).reshape(k // 32, 32, n)
    amax = np.abs(w).max(1)
    if fmt == "e4m3":
        byte = np.frexp(amax)[1] - 1 + 127 - 7
    else:
        mant, ex = np.frexp(amax / 6.0)
        byte = np.where(mant > 0.5, ex, ex - 1) + 127
    byte = np.clip(np.where(amax > 0, byte, 1), 1, 254)
    scaled = (w * np.exp2(127.0 - byte)[:, None, :]).reshape(k, n).astype(np.float32)
    by_word = np.ascontiguousarray(scaled.reshape(k // 512, 128, 4, n).transpose(0, 1, 3, 2))
    if fmt == "e4m3":
        words = by_word.astype(ml_dtypes.float8_e4m3fn).view(np.uint8)
    else:
        c = by_word.astype(ml_dtypes.float4_e2m1fn).view(np.uint8) & 0xF
        words = c[..., 0::2] | (c[..., 1::2] << 4)
    return np.ascontiguousarray(words), np.ascontiguousarray(byte.astype(np.uint8).reshape(k // 512, 16, n))


def unpack_weight(words, scales, fmt):
    g, p, n, _ = words.shape
    if fmt == "e4m3":
        vals = np.ascontiguousarray(words).view(ml_dtypes.float8_e4m3fn).astype(np.float64)
    else:
        nib = np.empty((g, p, n, 4), np.uint8)
        nib[..., 0::2] = words & 0xF
        nib[..., 1::2] = words >> 4
        vals = E2M1[nib]
    vals = vals * np.repeat(np.exp2(scales.astype(np.float64) - 127.0), 8, axis=1)[..., None]
    return vals.transpose(0, 1, 3, 2).reshape(g * 512, n)


G1, G2, B, DIM, K, N = 4, 4, 16, 2, 8192, 512
FMT = "e4m3"


def sigmoid(v):
    return 1.0 / (1.0 + np.exp(-v))


def setup_inputs():
    s = mx_kscale(K)
    a = 1.5 / np.sqrt(K)
    r = np.random.standard_normal
    x = bf(r((G1, G2, B, K)) * s)
    wf = bf(r((DIM, K, N)) * a)
    uf = bf(r((DIM, DIM, N)) * 0.5)
    biasf = bf(r((DIM, N)) * 0.5)
    wi = bf(r((K, N)) * a)
    ui = bf(r((DIM, N)) * 0.5)
    biasi = bf(r(N) * 0.5)
    wo_words, wo_scales = pack_weight(r((K, N)) * a / s[:, None], FMT)
    uo = bf(r((DIM, N)) * 0.5)
    biaso = bf(r(N) * 0.5)
    wc_words, wc_scales = pack_weight(r((K, N)) * a / s[:, None], FMT)
    uc = bf(r((DIM, N)) * 0.5)
    biasc = bf(r(N) * 0.5)
    return {
        "x": x,
        "wf": wf,
        "uf": uf,
        "biasf": biasf,
        "wi": wi,
        "ui": ui,
        "biasi": biasi,
        "wo_words": wo_words,
        "wo_scales": wo_scales,
        "uo": uo,
        "biaso": biaso,
        "wc_words": wc_words,
        "wc_scales": wc_scales,
        "uc": uc,
        "biasc": biasc,
    }


def reference(x, wf, uf, biasf, wi, ui, biasi, wo_words, wo_scales, uo, biaso, wc_words, wc_scales, uc, biasc):
    xq = mxq(f64(x), 3, "e4m3")
    o = sigmoid((xq @ unpack_weight(wo_words, wo_scales, FMT)) + f64(biaso))
    c = sigmoid((xq @ unpack_weight(wc_words, wc_scales, FMT)) + f64(biasc))
    return o * np.tanh(c)

@@ -1,0 +1,182 @@
+from contextlib import ExitStack
+
+import concourse.mybir as mybir
+from concourse.masks import make_identity
+
+F32 = mybir.dt.float32
+BF16 = mybir.dt.bfloat16
+I32 = mybir.dt.int32
+U32 = mybir.dt.uint32
+U8 = mybir.dt.uint8
+FP8X4 = mybir.dt.float8_e4m3fn_x4
+ACT = mybir.ActivationFunctionType
+
+P = 128
+PACK = 4
+K_GROUP = P * PACK
+ROWS = 256
+ROW_TILES = ROWS // P
+K = 8192
+GROUPS = K // K_GROUP
+N = 512
+
+CHUNK_GROUPS = 4
+CHUNKS = GROUPS // CHUNK_GROUPS
+CHUNK_K = CHUNK_GROUPS * K_GROUP
+GROUP_WORDS = K_GROUP // 2
+BANK_GROUPS = 2
+
+CELL, OUTPUT = 0, 1
+QUADRANTS = 4
+SHARED = 4
+SLOTS = GROUPS // SHARED
+SCALE_LOADS = 2 * SLOTS * QUADRANTS
+
+FLOPS = 2 * 2 * ROWS * K * N
+BYTES = 2 * ROWS * K + 2 * (K * N + K * N // 32) + 2 * 2 * N + 4 * ROWS * N
+
+
+def tile_mdlstm_k_kernel(
+    tc, x, wf, uf, biasf, wi, ui, biasi, wo_words, wo_scales, uo, biaso, wc_words, wc_scales, uc, biasc, out
+):
+    nc = tc.nc
+    x_rows = x.rearrange("a b c k -> (a b c) k")
+    out_rows = out.rearrange("a b c n -> (a b c) n")
+    given_words = (wc_words, wo_words)
+    given_scales = (wc_scales, wo_scales)
+    given_bias = (biasc, biaso)
+
+    with ExitStack() as ctx:
+        ctx.enter_context(tc.manual_schedule())
+        const = ctx.enter_context(tc.tile_pool(name="const", bufs=1))
+        x_pool = ctx.enter_context(tc.tile_pool(name="x", bufs=1))
+        w_pool = ctx.enter_context(tc.tile_pool(name="w", bufs=1))
+        code_pool = ctx.enter_context(tc.tile_pool(name="codes", bufs=1))
+        stage = ctx.enter_context(tc.tile_pool(name="stage", bufs=4))
+        tail = ctx.enter_context(tc.tile_pool(name="tail", bufs=1))
+        psum_t = ctx.enter_context(tc.psum_pool(name="psum_t", bufs=4))
+        psum_acc = ctx.enter_context(tc.psum_pool(name="psum_acc", bufs=1))
+
+        scale_planes = const.tile([P, 2 * SLOTS * N], U8, align_bytes=64)
+        nc.vector.memset(scale_planes[:].bitcast(I32), 0)
+        bias_rows = const.tile([P, 2, N], BF16)
+        nc.vector.memset(bias_rows[:], 0.0)
+        ones = const.tile([P, P], BF16)
+        nc.vector.memset(ones[:], 1.0)
+        identity = const.tile([P, P], F32)
+        make_identity(nc, identity[:])
+        for w in (CELL, OUTPUT):
+            nc.scalar.dma_start(out=bias_rows[0:1, w, :], in_=given_bias[w].unsqueeze(0))
+
+        def plane_columns(w, g):
+            first = (w * SLOTS + g // SHARED) * N
+            return slice(first, first + N)
+
+        def load_scale_rows(i):
+            w, s, quadrant = i // (SLOTS * QUADRANTS), (i // QUADRANTS) % SLOTS, i % QUADRANTS
+            nc.sync.dma_start(
+                out=scale_planes[32 * quadrant : 32 * quadrant + 4 * SHARED, plane_columns(w, s * SHARED)].bitcast(I32),
+                in_=given_scales[w][s * SHARED : (s + 1) * SHARED, 4 * quadrant : 4 * quadrant + 4, :].bitcast(I32),
+            )
+
+        large_loads = 0
+        x_chunks = {}
+        for c in range(CHUNKS):
+            for r in range(ROW_TILES):
+                x_chunk = x_pool.tile([P, CHUNK_K], BF16, name="x_chunk_%d_%d" % (c, r))
+                nc.sync.dma_start(out=x_chunk[:], in_=x_rows[r * P : (r + 1) * P, c * CHUNK_K : (c + 1) * CHUNK_K])
+                x_chunks[(c, r)] = x_chunk
+                load_scale_rows(large_loads)
+                large_loads += 1
+        w_words = {}
+        for w in (CELL, OUTPUT):
+            for g in range(GROUPS):
+                words = w_pool.tile([P, N], U32, name="words_%d_%d" % (w, g), align_bytes=64)
+                nc.sync.dma_start(
+                    out=words[:].bitcast(I32), in_=given_words[w][g].rearrange("p n t -> p (n t)").bitcast(I32)
+                )
+                w_words[(w, g)] = words
+                if large_loads < SCALE_LOADS:
+                    load_scale_rows(large_loads)
+                large_loads += 1
+
+        x_codes = {}
+        x_scales = {}
+
+        def quantise(c, r, grouped):
+            codes = code_pool.tile([P, CHUNK_GROUPS, P], U32, name="x_codes_%d_%d" % (c, r), align_bytes=64)
+            scales = code_pool.tile([P, CHUNK_GROUPS, P], U8, name="x_scales_%d_%d" % (c, r), align_bytes=64)
+            nc.vector.quantize_mx(
+                out=codes[:].rearrange("p g m -> p (g m)").bitcast(FP8X4),
+                scales=scales[:].rearrange("p g m -> p (g m)"),
+                in_=grouped[:].rearrange("p g m t -> p (g m t)"),
+            )
+            x_codes[(c, r)] = codes
+            x_scales[(c, r)] = scales
+
+        banks = 0
+        waiting = None
+        for c in range(CHUNKS):
+            for r in range(ROW_TILES):
+                x_words = x_chunks[(c, r)][:].bitcast(F32)
+                grouped = stage.tile([P, CHUNK_GROUPS, P, PACK], BF16, align_bytes=64)
+                for b in range(CHUNK_GROUPS // BANK_GROUPS):
+                    transposed = psum_t.tile([P, BANK_GROUPS, 2, P], F32, tag="bank")
+                    for j in range(BANK_GROUPS):
+                        first = (b * BANK_GROUPS + j) * GROUP_WORDS
+                        for u in range(2):
+                            nc.tensor.transpose(
+                                transposed[:, j, u, :], x_words[:, first + u : first + GROUP_WORDS : 2], identity[:]
+                            )
+                    copy = nc.vector.tensor_copy if banks % 4 == 3 else nc.scalar.copy
+                    copy(
+                        out=grouped[:, b * BANK_GROUPS : (b + 1) * BANK_GROUPS, :, :].bitcast(F32),
+                        in_=transposed[:].rearrange("p j u m -> p j m u"),
+                    )
+                    banks += 1
+                if waiting is not None:
+                    quantise(*waiting)
+                waiting = (c, r, grouped)
+        quantise(*waiting)
+
+        bias_all = const.tile([P, 2, N], F32)
+        for w in (CELL, OUTPUT):
+            repeated = psum_t.tile([P, N], F32, tag="bank")
+            nc.tensor.matmul(repeated[:], lhsT=ones[:], rhs=bias_rows[:, w, :], start=True, stop=True)
+            nc.scalar.copy(out=bias_all[:, w, :], in_=repeated[:])
+
+        def gate(w):
+            sums = [psum_acc.tile([P, N], F32, name="sums_%d_%d" % (w, r)) for r in range(ROW_TILES)]
+            for g in range(GROUPS):
+                c, j = g // CHUNK_GROUPS, g % CHUNK_GROUPS
+                for r in range(ROW_TILES):
+                    nc.tensor.matmul_mx(
+                        out=sums[r][:],
+                        lhsT=x_codes[(c, r)][:, j, :].bitcast(FP8X4),
+                        lhsT_scale=x_scales[(c, r)][:, j, :],
+                        rhs=w_words[(w, g)][:].bitcast(FP8X4),
+                        rhs_scale=scale_planes[4 * (g % SHARED) : P, plane_columns(w, g)],
+                        start=(g == 0),
+                        stop=(g == GROUPS - 1),
+                    )
+            gates = []
+            for r in range(ROW_TILES):
+                biased = tail.tile([P, N], F32, name="biased_%d_%d" % (w, r))
+                nc.vector.tensor_add(out=biased[:], in0=sums[r][:], in1=bias_all[:, w, :])
+                squashed = tail.tile([P, N], F32, name="gate_%d_%d" % (w, r))
+                nc.scalar.activation(out=squashed[:], in_=biased[:], func=ACT.Sigmoid)
+                gates.append(squashed)
+            return gates
+
+        cell = gate(CELL)
+        tanh_cell = []
+        for r in range(ROW_TILES):
+            squashed = tail.tile([P, N], F32, name="tanh_cell_%d" % r)
+            nc.scalar.activation(out=squashed[:], in_=cell[r][:], func=ACT.Tanh)
+            tanh_cell.append(squashed)
+
+        output = gate(OUTPUT)
+        for r in range(ROW_TILES):
+            result = tail.tile([P, N], F32, name="result_%d" % r)
+            nc.vector.tensor_mul(out=result[:], in0=output[r][:], in1=tanh_cell[r][:])
+            nc.sync.dma_start(out=out_rows[r * P : (r + 1) * P, :], in_=result[:])

@@ -30,7 +30,7 @@ CELL, OUTPUT = 0, 1
 QUADRANTS = 4
 SHARED = 4
 SLOTS = GROUPS // SHARED
-SCALE_LOADS = 2 * SLOTS * QUADRANTS
+SCALE_LOADS = SLOTS * QUADRANTS
 
 FLOPS = 2 * 2 * ROWS * K * N
 BYTES = 2 * ROWS * K + 2 * (K * N + K * N // 32) + 2 * 2 * N + 4 * ROWS * N
@@ -72,12 +72,15 @@ def tile_mdlstm_k_kernel(
             first = (w * SLOTS + g // SHARED) * N
             return slice(first, first + N)
 
-        def load_scale_rows(i):
-            w, s, quadrant = i // (SLOTS * QUADRANTS), (i // QUADRANTS) % SLOTS, i % QUADRANTS
-            nc.sync.dma_start(
-                out=scale_planes[32 * quadrant : 32 * quadrant + 4 * SHARED, plane_columns(w, s * SHARED)].bitcast(I32),
-                in_=given_scales[w][s * SHARED : (s + 1) * SHARED, 4 * quadrant : 4 * quadrant + 4, :].bitcast(I32),
+        def load_scale_rows(queue, view, w, i):
+            s, quadrant = i // QUADRANTS, i % QUADRANTS
+            queue.dma_start(
+                out=scale_planes[32 * quadrant : 32 * quadrant + 4 * SHARED, plane_columns(w, s * SHARED)].bitcast(view),
+                in_=given_scales[w][s * SHARED : (s + 1) * SHARED, 4 * quadrant : 4 * quadrant + 4, :].bitcast(view),
             )
+
+        for i in range(SCALE_LOADS):
+            load_scale_rows(nc.gpsimd, F32, OUTPUT, i)
 
         large_loads = 0
         x_chunks = {}
@@ -86,7 +89,7 @@ def tile_mdlstm_k_kernel(
                 x_chunk = x_pool.tile([P, CHUNK_K], BF16, name="x_chunk_%d_%d" % (c, r))
                 nc.sync.dma_start(out=x_chunk[:], in_=x_rows[r * P : (r + 1) * P, c * CHUNK_K : (c + 1) * CHUNK_K])
                 x_chunks[(c, r)] = x_chunk
-                load_scale_rows(large_loads)
+                load_scale_rows(nc.sync, I32, CELL, large_loads)
                 large_loads += 1
         w_words = {}
         for w in (CELL, OUTPUT):
@@ -97,7 +100,7 @@ def tile_mdlstm_k_kernel(
                 )
                 w_words[(w, g)] = words
                 if large_loads < SCALE_LOADS:
-                    load_scale_rows(large_loads)
+                    load_scale_rows(nc.sync, I32, CELL, large_loads)
                 large_loads += 1
 
         x_codes = {}

@@ -19,6 +19,10 @@ ROW_TILES = ROWS // P
 K = 8192
 GROUPS = K // K_GROUP
 N = 512
+HALVES = 2
+HALF = N // HALVES
+LATE_GROUPS = 3
+WHOLE = (0, N)
 
 CHUNK_GROUPS = 4
 CHUNKS = GROUPS // CHUNK_GROUPS
@@ -30,7 +34,6 @@ CELL, OUTPUT = 0, 1
 QUADRANTS = 4
 SHARED = 4
 SLOTS = GROUPS // SHARED
-SCALE_LOADS = SLOTS * QUADRANTS
 
 FLOPS = 2 * 2 * ROWS * K * N
 BYTES = 2 * ROWS * K + 2 * (K * N + K * N // 32) + 2 * 2 * N + 4 * ROWS * N
@@ -42,7 +45,6 @@ def tile_mdlstm_k_kernel(
     nc = tc.nc
     x_rows = x.rearrange("a b c k -> (a b c) k")
     out_rows = out.rearrange("a b c n -> (a b c) n")
-    given_words = (wc_words, wo_words)
     given_scales = (wc_scales, wo_scales)
     given_bias = (biasc, biaso)
 
@@ -54,8 +56,8 @@ def tile_mdlstm_k_kernel(
         code_pool = ctx.enter_context(tc.tile_pool(name="codes", bufs=1))
         stage = ctx.enter_context(tc.tile_pool(name="stage", bufs=4))
         tail = ctx.enter_context(tc.tile_pool(name="tail", bufs=1))
-        psum_t = ctx.enter_context(tc.psum_pool(name="psum_t", bufs=4))
-        psum_acc = ctx.enter_context(tc.psum_pool(name="psum_acc", bufs=1))
+        psum_turn = ctx.enter_context(tc.psum_pool(name="psum_turn", bufs=4))
+        psum_cell = ctx.enter_context(tc.psum_pool(name="psum_cell", bufs=1))
 
         scale_planes = const.tile([P, 2 * SLOTS * N], U8, align_bytes=64)
         nc.vector.memset(scale_planes[:].bitcast(I32), 0)
@@ -68,40 +70,52 @@ def tile_mdlstm_k_kernel(
         for w in (CELL, OUTPUT):
             nc.scalar.dma_start(out=bias_rows[0:1, w, :], in_=given_bias[w].unsqueeze(0))
 
-        def plane_columns(w, g):
-            first = (w * SLOTS + g // SHARED) * N
-            return slice(first, first + N)
+        def plane(w, g, columns):
+            first, width = columns
+            first += (w * SLOTS + g // SHARED) * N
+            return scale_planes[4 * (g % SHARED) : P, first : first + width]
 
-        def load_scale_rows(queue, view, w, i):
-            s, quadrant = i // QUADRANTS, i % QUADRANTS
+        def load_scale_rows(queue, view, w, s, quadrant):
+            first = (w * SLOTS + s) * N
             queue.dma_start(
-                out=scale_planes[32 * quadrant : 32 * quadrant + 4 * SHARED, plane_columns(w, s * SHARED)].bitcast(view),
+                out=scale_planes[32 * quadrant : 32 * quadrant + 4 * SHARED, first : first + N].bitcast(view),
                 in_=given_scales[w][s * SHARED : (s + 1) * SHARED, 4 * quadrant : 4 * quadrant + 4, :].bitcast(view),
             )
 
-        for i in range(SCALE_LOADS):
-            load_scale_rows(nc.gpsimd, F32, OUTPUT, i)
+        def load_words(given, g, columns, name):
+            first, width = columns
+            words = w_pool.tile([P, width], U32, name=name, align_bytes=64)
+            nc.sync.dma_start(
+                out=words[:].bitcast(I32),
+                in_=given[g].rearrange("p n t -> p (n t)").bitcast(I32)[:, first : first + width],
+            )
+            return words
 
-        large_loads = 0
+        for s in range(SLOTS):
+            for quadrant in range(QUADRANTS):
+                load_scale_rows(nc.gpsimd, F32, OUTPUT, s, quadrant)
+
         x_chunks = {}
         for c in range(CHUNKS):
             for r in range(ROW_TILES):
                 x_chunk = x_pool.tile([P, CHUNK_K], BF16, name="x_chunk_%d_%d" % (c, r))
                 nc.sync.dma_start(out=x_chunk[:], in_=x_rows[r * P : (r + 1) * P, c * CHUNK_K : (c + 1) * CHUNK_K])
                 x_chunks[(c, r)] = x_chunk
-                load_scale_rows(nc.sync, I32, CELL, large_loads)
-                large_loads += 1
-        w_words = {}
-        for w in (CELL, OUTPUT):
-            for g in range(GROUPS):
-                words = w_pool.tile([P, N], U32, name="words_%d_%d" % (w, g), align_bytes=64)
-                nc.sync.dma_start(
-                    out=words[:].bitcast(I32), in_=given_words[w][g].rearrange("p n t -> p (n t)").bitcast(I32)
-                )
-                w_words[(w, g)] = words
-                if large_loads < SCALE_LOADS:
-                    load_scale_rows(nc.sync, I32, CELL, large_loads)
-                large_loads += 1
+        wc_group = {}
+        for s in range(SLOTS):
+            for quadrant in range(QUADRANTS):
+                load_scale_rows(nc.sync, I32, CELL, s, quadrant)
+            for g in range(s * SHARED, (s + 1) * SHARED):
+                wc_group[g] = load_words(wc_words, g, WHOLE, "wc_%d" % g)
+        halves = [(h * HALF, HALF) for h in range(HALVES)]
+        wo_half = {}
+        for g in range(GROUPS - LATE_GROUPS):
+            whole = load_words(wo_words, g, WHOLE, "wo_%d" % g)
+            for h in range(HALVES):
+                wo_half[(g, h)] = whole[:, h * HALF : (h + 1) * HALF]
+        for h in range(HALVES):
+            for g in range(GROUPS - LATE_GROUPS, GROUPS):
+                wo_half[(g, h)] = load_words(wo_words, g, halves[h], "wo_%d_%d" % (g, h))[:]
 
         x_codes = {}
         x_scales = {}
@@ -124,7 +138,7 @@ def tile_mdlstm_k_kernel(
                 x_words = x_chunks[(c, r)][:].bitcast(F32)
                 grouped = stage.tile([P, CHUNK_GROUPS, P, PACK], BF16, align_bytes=64)
                 for b in range(CHUNK_GROUPS // BANK_GROUPS):
-                    transposed = psum_t.tile([P, BANK_GROUPS, 2, P], F32, tag="bank")
+                    transposed = psum_turn.tile([P, BANK_GROUPS, 2, P], F32, tag="bank")
                     for j in range(BANK_GROUPS):
                         first = (b * BANK_GROUPS + j) * GROUP_WORDS
                         for u in range(2):
@@ -144,42 +158,61 @@ def tile_mdlstm_k_kernel(
 
         bias_all = const.tile([P, 2, N], F32)
         for w in (CELL, OUTPUT):
-            repeated = psum_t.tile([P, N], F32, tag="bank")
+            repeated = psum_turn.tile([P, N], F32, tag="bank")
             nc.tensor.matmul(repeated[:], lhsT=ones[:], rhs=bias_rows[:, w, :], start=True, stop=True)
             nc.scalar.copy(out=bias_all[:, w, :], in_=repeated[:])
 
-        def gate(w):
-            sums = [psum_acc.tile([P, N], F32, name="sums_%d_%d" % (w, r)) for r in range(ROW_TILES)]
-            for g in range(GROUPS):
-                c, j = g // CHUNK_GROUPS, g % CHUNK_GROUPS
-                for r in range(ROW_TILES):
-                    nc.tensor.matmul_mx(
-                        out=sums[r][:],
-                        lhsT=x_codes[(c, r)][:, j, :].bitcast(FP8X4),
-                        lhsT_scale=x_scales[(c, r)][:, j, :],
-                        rhs=w_words[(w, g)][:].bitcast(FP8X4),
-                        rhs_scale=scale_planes[4 * (g % SHARED) : P, plane_columns(w, g)],
-                        start=(g == 0),
-                        stop=(g == GROUPS - 1),
-                    )
-            gates = []
-            for r in range(ROW_TILES):
-                biased = tail.tile([P, N], F32, name="biased_%d_%d" % (w, r))
-                nc.vector.tensor_add(out=biased[:], in0=sums[r][:], in1=bias_all[:, w, :])
-                squashed = tail.tile([P, N], F32, name="gate_%d_%d" % (w, r))
-                nc.scalar.activation(out=squashed[:], in_=biased[:], func=ACT.Sigmoid)
-                gates.append(squashed)
-            return gates
+        def multiply(sums, r, w, g, columns, words):
+            c, j = g // CHUNK_GROUPS, g % CHUNK_GROUPS
+            nc.tensor.matmul_mx(
+                out=sums[:],
+                lhsT=x_codes[(c, r)][:, j, :].bitcast(FP8X4),
+                lhsT_scale=x_scales[(c, r)][:, j, :],
+                rhs=words.bitcast(FP8X4),
+                rhs_scale=plane(w, g, columns),
+                start=(g == 0),
+                stop=(g == GROUPS - 1),
+            )
 
-        cell = gate(CELL)
+        def gate(sums, w, columns, name):
+            first, width = columns
+            biased = tail.tile([P, width], F32, name="biased_" + name)
+            nc.vector.tensor_add(out=biased[:], in0=sums[:], in1=bias_all[:, w, first : first + width])
+            squashed = tail.tile([P, width], F32, name="gate_" + name)
+            nc.scalar.activation(out=squashed[:], in_=biased[:], func=ACT.Sigmoid)
+            return squashed
+
+        cell_sums = [psum_cell.tile([P, N], F32, name="cell_sums_%d" % r) for r in range(ROW_TILES)]
+        for g in range(GROUPS):
+            for r in range(ROW_TILES):
+                multiply(cell_sums[r], r, CELL, g, WHOLE, wc_group[g][:])
         tanh_cell = []
         for r in range(ROW_TILES):
+            cell = gate(cell_sums[r], CELL, WHOLE, "cell_%d" % r)
             squashed = tail.tile([P, N], F32, name="tanh_cell_%d" % r)
-            nc.scalar.activation(out=squashed[:], in_=cell[r][:], func=ACT.Tanh)
+            nc.scalar.activation(out=squashed[:], in_=cell[:], func=ACT.Tanh)
             tanh_cell.append(squashed)
 
-        output = gate(OUTPUT)
-        for r in range(ROW_TILES):
-            result = tail.tile([P, N], F32, name="result_%d" % r)
-            nc.vector.tensor_mul(out=result[:], in0=output[r][:], in1=tanh_cell[r][:])
-            nc.sync.dma_start(out=out_rows[r * P : (r + 1) * P, :], in_=result[:])
+        output_sums = {}
+        for h in range(HALVES):
+            for r in range(ROW_TILES):
+                output_sums[(h, r)] = psum_turn.tile([P, HALF], F32, tag="bank", name="output_sums_%d_%d" % (h, r))
+        for g in range(GROUPS - LATE_GROUPS):
+            for h in range(HALVES):
+                for r in range(ROW_TILES):
+                    multiply(output_sums[(h, r)], r, OUTPUT, g, halves[h], wo_half[(g, h)])
+        for h in range(HALVES):
+            for g in range(GROUPS - LATE_GROUPS, GROUPS):
+                for r in range(ROW_TILES):
+                    multiply(output_sums[(h, r)], r, OUTPUT, g, halves[h], wo_half[(g, h)])
+
+        output = {}
+        for h in range(HALVES):
+            for r in range(ROW_TILES):
+                output[(h, r)] = gate(output_sums[(h, r)], OUTPUT, halves[h], "output_%d_%d" % (h, r))
+        for h in range(HALVES):
+            for r in range(ROW_TILES):
+                result = tail.tile([P, HALF], F32, name="result_%d_%d" % (h, r))
+                first, width = halves[h]
+                nc.vector.tensor_mul(out=result[:], in0=output[(h, r)][:], in1=tanh_cell[r][:, first : first + width])
+                nc.sync.dma_start(out=out_rows[r * P : (r + 1) * P, first : first + width], in_=result[:])

@@ -30,6 +30,9 @@ CHUNK_K = CHUNK_GROUPS * K_GROUP
 GROUP_WORDS = K_GROUP // 2
 BANK_GROUPS = 2
 
+BIAS_CHUNK = 2
+BIAS_GROUP = 7
+
 CELL, OUTPUT = 0, 1
 QUADRANTS = 4
 SHARED = 4
@@ -67,8 +70,6 @@ def tile_mdlstm_k_kernel(
         nc.vector.memset(ones[:], 1.0)
         identity = const.tile([P, P], F32)
         make_identity(nc, identity[:])
-        for w in (CELL, OUTPUT):
-            nc.scalar.dma_start(out=bias_rows[0:1, w, :], in_=given_bias[w].unsqueeze(0))
 
         def plane(w, g, columns):
             first, width = columns
@@ -91,20 +92,24 @@ def tile_mdlstm_k_kernel(
             )
             return words
 
-        for s in range(SLOTS):
+        for w, s in [(CELL, 2), (CELL, 3), (OUTPUT, 0), (OUTPUT, 1), (OUTPUT, 2), (OUTPUT, 3)]:
             for quadrant in range(QUADRANTS):
-                load_scale_rows(nc.gpsimd, F32, OUTPUT, s, quadrant)
+                load_scale_rows(nc.gpsimd, F32, w, s, quadrant)
 
         x_chunks = {}
         for c in range(CHUNKS):
+            if c == BIAS_CHUNK:
+                for w in (CELL, OUTPUT):
+                    nc.sync.dma_start(out=bias_rows[0:1, w, :], in_=given_bias[w].unsqueeze(0))
             for r in range(ROW_TILES):
                 x_chunk = x_pool.tile([P, CHUNK_K], BF16, name="x_chunk_%d_%d" % (c, r))
                 nc.sync.dma_start(out=x_chunk[:], in_=x_rows[r * P : (r + 1) * P, c * CHUNK_K : (c + 1) * CHUNK_K])
                 x_chunks[(c, r)] = x_chunk
         wc_group = {}
         for s in range(SLOTS):
-            for quadrant in range(QUADRANTS):
-                load_scale_rows(nc.sync, I32, CELL, s, quadrant)
+            if s < 2:
+                for quadrant in range(QUADRANTS):
+                    load_scale_rows(nc.sync, I32, CELL, s, quadrant)
             for g in range(s * SHARED, (s + 1) * SHARED):
                 wc_group[g] = load_words(wc_words, g, WHOLE, "wc_%d" % g)
         halves = [(h * HALF, HALF) for h in range(HALVES)]
@@ -156,12 +161,6 @@ def tile_mdlstm_k_kernel(
                 waiting = (c, r, grouped)
         quantise(*waiting)
 
-        bias_all = const.tile([P, 2, N], F32)
-        for w in (CELL, OUTPUT):
-            repeated = psum_turn.tile([P, N], F32, tag="bank")
-            nc.tensor.matmul(repeated[:], lhsT=ones[:], rhs=bias_rows[:, w, :], start=True, stop=True)
-            nc.scalar.copy(out=bias_all[:, w, :], in_=repeated[:])
-
         def multiply(sums, r, w, g, columns, words):
             c, j = g // CHUNK_GROUPS, g % CHUNK_GROUPS
             nc.tensor.matmul_mx(
@@ -183,9 +182,15 @@ def tile_mdlstm_k_kernel(
             return squashed
 
         cell_sums = [psum_cell.tile([P, N], F32, name="cell_sums_%d" % r) for r in range(ROW_TILES)]
+        bias_all = const.tile([P, 2, N], F32)
         for g in range(GROUPS):
             for r in range(ROW_TILES):
                 multiply(cell_sums[r], r, CELL, g, WHOLE, wc_group[g][:])
+            if g == BIAS_GROUP:
+                for w in (CELL, OUTPUT):
+                    repeated = psum_turn.tile([P, N], F32, tag="bank")
+                    nc.tensor.matmul(repeated[:], lhsT=ones[:], rhs=bias_rows[:, w, :], start=True, stop=True)
+                    nc.scalar.copy(out=bias_all[:, w, :], in_=repeated[:])
         tanh_cell = []
         for r in range(ROW_TILES):
             cell = gate(cell_sums[r], CELL, WHOLE, "cell_%d" % r)

from contextlib import ExitStack

import concourse.mybir as mybir
from concourse.masks import make_identity

F32 = mybir.dt.float32
BF16 = mybir.dt.bfloat16
I32 = mybir.dt.int32
U32 = mybir.dt.uint32
U8 = mybir.dt.uint8
FP8X4 = mybir.dt.float8_e4m3fn_x4
ACT = mybir.ActivationFunctionType

P = 128
PACK = 4
K_GROUP = P * PACK
ROWS = 256
ROW_TILES = ROWS // P
K = 8192
GROUPS = K // K_GROUP
N = 512
HALVES = 2
HALF = N // HALVES
LATE_GROUPS = 3
WHOLE = (0, N)

CHUNK_GROUPS = 4
CHUNKS = GROUPS // CHUNK_GROUPS
CHUNK_K = CHUNK_GROUPS * K_GROUP
GROUP_WORDS = K_GROUP // 2
BANK_GROUPS = 2

BIAS_CHUNK = 2
BIAS_GROUP = 7

CELL, OUTPUT = 0, 1
QUADRANTS = 4
SHARED = 4
SLOTS = GROUPS // SHARED

FLOPS = 2 * 2 * ROWS * K * N
BYTES = 2 * ROWS * K + 2 * (K * N + K * N // 32) + 2 * 2 * N + 4 * ROWS * N


def tile_mdlstm_k_kernel(
    tc, x, wf, uf, biasf, wi, ui, biasi, wo_words, wo_scales, uo, biaso, wc_words, wc_scales, uc, biasc, out
):
    nc = tc.nc
    x_rows = x.rearrange("a b c k -> (a b c) k")
    out_rows = out.rearrange("a b c n -> (a b c) n")
    given_scales = (wc_scales, wo_scales)
    given_bias = (biasc, biaso)

    with ExitStack() as ctx:
        ctx.enter_context(tc.manual_schedule())
        const = ctx.enter_context(tc.tile_pool(name="const", bufs=1))
        x_pool = ctx.enter_context(tc.tile_pool(name="x", bufs=1))
        w_pool = ctx.enter_context(tc.tile_pool(name="w", bufs=1))
        code_pool = ctx.enter_context(tc.tile_pool(name="codes", bufs=1))
        stage = ctx.enter_context(tc.tile_pool(name="stage", bufs=4))
        tail = ctx.enter_context(tc.tile_pool(name="tail", bufs=1))
        psum_turn = ctx.enter_context(tc.psum_pool(name="psum_turn", bufs=4))
        psum_cell = ctx.enter_context(tc.psum_pool(name="psum_cell", bufs=1))

        scale_planes = const.tile([P, 2 * SLOTS * N], U8, align_bytes=64)
        nc.vector.memset(scale_planes[:].bitcast(I32), 0)
        bias_rows = const.tile([P, 2, N], BF16)
        nc.vector.memset(bias_rows[:], 0.0)
        ones = const.tile([P, P], BF16)
        nc.vector.memset(ones[:], 1.0)
        identity = const.tile([P, P], F32)
        make_identity(nc, identity[:])

        def plane(w, g, columns):
            first, width = columns
            first += (w * SLOTS + g // SHARED) * N
            return scale_planes[4 * (g % SHARED) : P, first : first + width]

        def load_scale_rows(queue, view, w, s, quadrant):
            first = (w * SLOTS + s) * N
            queue.dma_start(
                out=scale_planes[32 * quadrant : 32 * quadrant + 4 * SHARED, first : first + N].bitcast(view),
                in_=given_scales[w][s * SHARED : (s + 1) * SHARED, 4 * quadrant : 4 * quadrant + 4, :].bitcast(view),
            )

        def load_words(given, g, columns, name):
            first, width = columns
            words = w_pool.tile([P, width], U32, name=name, align_bytes=64)
            nc.sync.dma_start(
                out=words[:].bitcast(I32),
                in_=given[g].rearrange("p n t -> p (n t)").bitcast(I32)[:, first : first + width],
            )
            return words

        for w, s in [(CELL, 2), (CELL, 3), (OUTPUT, 0), (OUTPUT, 1), (OUTPUT, 2), (OUTPUT, 3)]:
            for quadrant in range(QUADRANTS):
                load_scale_rows(nc.gpsimd, F32, w, s, quadrant)

        x_chunks = {}
        for c in range(CHUNKS):
            if c == BIAS_CHUNK:
                for w in (CELL, OUTPUT):
                    nc.sync.dma_start(out=bias_rows[0:1, w, :], in_=given_bias[w].unsqueeze(0))
            for r in range(ROW_TILES):
                x_chunk = x_pool.tile([P, CHUNK_K], BF16, name="x_chunk_%d_%d" % (c, r))
                nc.sync.dma_start(out=x_chunk[:], in_=x_rows[r * P : (r + 1) * P, c * CHUNK_K : (c + 1) * CHUNK_K])
                x_chunks[(c, r)] = x_chunk
        wc_group = {}
        for s in range(SLOTS):
            if s < 2:
                for quadrant in range(QUADRANTS):
                    load_scale_rows(nc.sync, I32, CELL, s, quadrant)
            for g in range(s * SHARED, (s + 1) * SHARED):
                wc_group[g] = load_words(wc_words, g, WHOLE, "wc_%d" % g)
        halves = [(h * HALF, HALF) for h in range(HALVES)]
        wo_half = {}
        for g in range(GROUPS - LATE_GROUPS):
            whole = load_words(wo_words, g, WHOLE, "wo_%d" % g)
            for h in range(HALVES):
                wo_half[(g, h)] = whole[:, h * HALF : (h + 1) * HALF]
        for h in range(HALVES):
            for g in range(GROUPS - LATE_GROUPS, GROUPS):
                wo_half[(g, h)] = load_words(wo_words, g, halves[h], "wo_%d_%d" % (g, h))[:]

        x_codes = {}
        x_scales = {}

        def quantise(c, r, grouped):
            codes = code_pool.tile([P, CHUNK_GROUPS, P], U32, name="x_codes_%d_%d" % (c, r), align_bytes=64)
            scales = code_pool.tile([P, CHUNK_GROUPS, P], U8, name="x_scales_%d_%d" % (c, r), align_bytes=64)
            nc.vector.quantize_mx(
                out=codes[:].rearrange("p g m -> p (g m)").bitcast(FP8X4),
                scales=scales[:].rearrange("p g m -> p (g m)"),
                in_=grouped[:].rearrange("p g m t -> p (g m t)"),
            )
            x_codes[(c, r)] = codes
            x_scales[(c, r)] = scales

        banks = 0
        waiting = None
        for c in range(CHUNKS):
            for r in range(ROW_TILES):
                x_words = x_chunks[(c, r)][:].bitcast(F32)
                grouped = stage.tile([P, CHUNK_GROUPS, P, PACK], BF16, align_bytes=64)
                for b in range(CHUNK_GROUPS // BANK_GROUPS):
                    transposed = psum_turn.tile([P, BANK_GROUPS, 2, P], F32, tag="bank")
                    for j in range(BANK_GROUPS):
                        first = (b * BANK_GROUPS + j) * GROUP_WORDS
                        for u in range(2):
                            nc.tensor.transpose(
                                transposed[:, j, u, :], x_words[:, first + u : first + GROUP_WORDS : 2], identity[:]
                            )
                    copy = nc.vector.tensor_copy if banks % 4 == 3 else nc.scalar.copy
                    copy(
                        out=grouped[:, b * BANK_GROUPS : (b + 1) * BANK_GROUPS, :, :].bitcast(F32),
                        in_=transposed[:].rearrange("p j u m -> p j m u"),
                    )
                    banks += 1
                if waiting is not None:
                    quantise(*waiting)
                waiting = (c, r, grouped)
        quantise(*waiting)

        def multiply(sums, r, w, g, columns, words):
            c, j = g // CHUNK_GROUPS, g % CHUNK_GROUPS
            nc.tensor.matmul_mx(
                out=sums[:],
                lhsT=x_codes[(c, r)][:, j, :].bitcast(FP8X4),
                lhsT_scale=x_scales[(c, r)][:, j, :],
                rhs=words.bitcast(FP8X4),
                rhs_scale=plane(w, g, columns),
                start=(g == 0),
                stop=(g == GROUPS - 1),
            )

        def gate(sums, w, columns, name):
            first, width = columns
            biased = tail.tile([P, width], F32, name="biased_" + name)
            nc.vector.tensor_add(out=biased[:], in0=sums[:], in1=bias_all[:, w, first : first + width])
            squashed = tail.tile([P, width], F32, name="gate_" + name)
            nc.scalar.activation(out=squashed[:], in_=biased[:], func=ACT.Sigmoid)
            return squashed

        cell_sums = [psum_cell.tile([P, N], F32, name="cell_sums_%d" % r) for r in range(ROW_TILES)]
        bias_all = const.tile([P, 2, N], F32)
        for g in range(GROUPS):
            for r in range(ROW_TILES):
                multiply(cell_sums[r], r, CELL, g, WHOLE, wc_group[g][:])
            if g == BIAS_GROUP:
                for w in (CELL, OUTPUT):
                    repeated = psum_turn.tile([P, N], F32, tag="bank")
                    nc.tensor.matmul(repeated[:], lhsT=ones[:], rhs=bias_rows[:, w, :], start=True, stop=True)
                    nc.scalar.copy(out=bias_all[:, w, :], in_=repeated[:])
        tanh_cell = []
        for r in range(ROW_TILES):
            cell = gate(cell_sums[r], CELL, WHOLE, "cell_%d" % r)
            squashed = tail.tile([P, N], F32, name="tanh_cell_%d" % r)
            nc.scalar.activation(out=squashed[:], in_=cell[:], func=ACT.Tanh)
            tanh_cell.append(squashed)

        output_sums = {}
        for h in range(HALVES):
            for r in range(ROW_TILES):
                output_sums[(h, r)] = psum_turn.tile([P, HALF], F32, tag="bank", name="output_sums_%d_%d" % (h, r))
        for g in range(GROUPS - LATE_GROUPS):
            for h in range(HALVES):
                for r in range(ROW_TILES):
                    multiply(output_sums[(h, r)], r, OUTPUT, g, halves[h], wo_half[(g, h)])
        for h in range(HALVES):
            for g in range(GROUPS - LATE_GROUPS, GROUPS):
                for r in range(ROW_TILES):
                    multiply(output_sums[(h, r)], r, OUTPUT, g, halves[h], wo_half[(g, h)])

        output = {}
        for h in range(HALVES):
            for r in range(ROW_TILES):
                output[(h, r)] = gate(output_sums[(h, r)], OUTPUT, halves[h], "output_%d_%d" % (h, r))
        for h in range(HALVES):
            for r in range(ROW_TILES):
                result = tail.tile([P, HALF], F32, name="result_%d_%d" % (h, r))
                first, width = halves[h]
                nc.vector.tensor_mul(out=result[:], in0=output[(h, r)][:], in1=tanh_cell[r][:, first : first + width])
                nc.sync.dma_start(out=out_rows[r * P : (r + 1) * P, first : first + width], in_=result[:])
